import numpy as np
import ml_dtypes


BF16 = ml_dtypes.bfloat16


def bf(x):
    return np.asarray(x, np.float32).astype(BF16)


def f64(x):
    return np.asarray(x).astype(np.float64)


E2M1 = np.array([0.0, 0.5, 1.0, 1.5, 2.0, 3.0, 4.0, 6.0, -0.0, -0.5, -1.0, -1.5, -2.0, -3.0, -4.0, -6.0])


def pack_weight(w, fmt):
    k, n = w.shape
    w = f64(bf(w)).reshape(k // 32, 32, n)
    amax = np.abs(w).max(1)
    if fmt == "e4m3":
        byte = np.frexp(amax)[1] - 1 + 127 - 7
    else:
        mant, ex = np.frexp(amax / 6.0)
        byte = np.where(mant > 0.5, ex, ex - 1) + 127
    byte = np.clip(np.where(amax > 0, byte, 1), 1, 254)
    scaled = (w * np.exp2(127.0 - byte)[:, None, :]).reshape(k, n).astype(np.float32)
    by_word = np.ascontiguousarray(scaled.reshape(k // 512, 128, 4, n).transpose(0, 1, 3, 2))
    if fmt == "e4m3":
        words = by_word.astype(ml_dtypes.float8_e4m3fn).view(np.uint8)
    else:
        c = by_word.astype(ml_dtypes.float4_e2m1fn).view(np.uint8) & 0xF
        words = c[..., 0::2] | (c[..., 1::2] << 4)
    return np.ascontiguousarray(words), np.ascontiguousarray(byte.astype(np.uint8).reshape(k // 512, 16, n))


def unpack_weight(words, scales, fmt):
    g, p, n, _ = words.shape
    if fmt == "e4m3":
        vals = np.ascontiguousarray(words).view(ml_dtypes.float8_e4m3fn).astype(np.float64)
    else:
        nib = np.empty((g, p, n, 4), np.uint8)
        nib[..., 0::2] = words & 0xF
        nib[..., 1::2] = words >> 4
        vals = E2M1[nib]
    vals = vals * np.repeat(np.exp2(scales.astype(np.float64) - 127.0), 8, axis=1)[..., None]
    return vals.transpose(0, 1, 3, 2).reshape(g * 512, n)

def pack4(w):
    words, scales = pack_weight(w, "e2m1")
    return words.reshape(words.shape[0], 128, -1), scales


def unpack4(words, scales):
    return unpack_weight(words.reshape(words.shape[0], 128, -1, 2), scales, "e2m1")


def kspread(k):
    return np.exp2(np.repeat(np.random.randint(-6, 7, k // 32), 32).astype(np.float64))


B, S, K, N = 2, 1024, 2048, 4096


def setup_inputs():
    s = kspread(K)
    input = np.random.standard_normal((B, S, K)) * s
    input_words, input_scales = pack4(np.ascontiguousarray(input.reshape(B * S, K).T))
    weight = np.random.standard_normal((N, K)) / np.sqrt(K) / s[None, :]
    words, scales = pack4(np.ascontiguousarray(weight.T))
    bias = bf(np.random.standard_normal(N) * 0.5)
    return {"input_words": input_words,
            "input_scales": input_scales,
            "weight_words": words,
            "weight_scales": scales,
            "bias": bias}


def reference(input_words, input_scales, weight_words, weight_scales, bias):
    xq = unpack4(input_words, input_scales).T.reshape(B, S, K)
    wq = unpack4(weight_words, weight_scales)
    out = xq.reshape(B * S, K) @ wq
    return out.reshape(B, S, N) + f64(bias)

@@ -1,0 +1,171 @@
+from contextlib import ExitStack
+
+import concourse.mybir as mybir
+
+TOKENS, FEATURES, CHANNELS = 2048, 2048, 4096
+FLOPS = 2 * TOKENS * FEATURES * CHANNELS
+
+F32 = mybir.dt.float32
+BF16 = mybir.dt.bfloat16
+I32 = mybir.dt.int32
+U8 = mybir.dt.uint8
+FP4X4 = mybir.dt.float4_e2m1fn_x4
+
+P = 128
+PASSES = FEATURES // 512
+M_TILE = 128
+N_TILE = 512
+T_TILES = TOKENS // M_TILE
+C_BLOCKS = CHANNELS // N_TILE
+
+X_CHUNKS = ((0, 4), (4, 4), (8, 8))
+HEAD_TILES = X_CHUNKS[0][1]
+ALL_PASSES = ((0, PASSES),)
+HEAD_PASSES = ((0, 1), (1, 2), (2, PASSES))
+AHEAD = 2
+WARM_MATMULS = 6
+LAST_WIDTHS = (256, 256)
+
+
+def tile_tiledlinear_kernel(tc, input_words, input_scales, weight_words, weight_scales, bias, out):
+    nc = tc.nc
+    out_rows = out.flatten_outer_dims()
+
+    with ExitStack() as ctx:
+        keep = ctx.enter_context(tc.tile_pool(name="keep", bufs=1))
+        stage = ctx.enter_context(tc.tile_pool(name="stage", bufs=6))
+        psum = ctx.enter_context(tc.psum_pool(name="psum", bufs=8))
+        ctx.enter_context(tc.manual_schedule())
+
+        def code_tiles(name, width, pass_ranges):
+            return [
+                (g0, g1, keep.tile([P, g1 - g0, width], U8, name="%s_%d" % (name, g0), align_bytes=64))
+                for g0, g1 in pass_ranges
+            ]
+
+        def load_codes(tiles, i, words, b0):
+            g0, g1, codes = tiles[i]
+            nc.sync.dma_start(
+                out=codes[:].bitcast(I32),
+                in_=words[g0:g1, :, b0 : b0 + codes.shape[2]].rearrange("g p n -> p g n").bitcast(I32),
+            )
+
+        def codes_of_pass(tiles, g):
+            for g0, g1, codes in tiles:
+                if g0 <= g < g1:
+                    found = codes[:, g - g0, :]
+            return found
+
+        def plane_tile(name, width):
+            return keep.tile([P, PASSES, width], U8, name=name, align_bytes=64)
+
+        def zero_plane(plane):
+            nc.vector.memset(plane[:].bitcast(I32), 0)
+
+        def load_scales(plane, scales, n0):
+            for r in range(4):
+                nc.sync.dma_start(
+                    out=plane[r:P:32, :, :].bitcast(I32),
+                    in_=scales[:, r:16:4, n0 : n0 + plane.shape[2]].rearrange("g q n -> q g n").bitcast(I32),
+                )
+
+        x_codes = [
+            code_tiles("x_codes%d" % i, 2 * M_TILE * n, HEAD_PASSES if i == 0 else ALL_PASSES)
+            for i, (first, n) in enumerate(X_CHUNKS)
+        ]
+        x_planes = [plane_tile("x_plane%d" % i, M_TILE * n) for i, (first, n) in enumerate(X_CHUNKS)]
+        w_codes = [
+            code_tiles("w_codes%d" % c, 2 * N_TILE, HEAD_PASSES if c == 0 else ALL_PASSES) for c in range(C_BLOCKS)
+        ]
+        w_planes = [plane_tile("w_plane%d" % c, N_TILE) for c in range(C_BLOCKS)]
+        bias_all = [keep.tile([P, N_TILE], BF16, name="bias%d" % c) for c in range(C_BLOCKS)]
+        zeros = keep.tile([P, N_TILE], BF16, name="zeros")
+
+        def load_x_codes(i, j):
+            load_codes(x_codes[i], j, input_words, 2 * M_TILE * X_CHUNKS[i][0])
+
+        def load_x_scales(i):
+            load_scales(x_planes[i], input_scales, M_TILE * X_CHUNKS[i][0])
+
+        def load_w_codes(c, j):
+            load_codes(w_codes[c], j, weight_words, 2 * N_TILE * c)
+
+        def load_w_scales(c):
+            load_scales(w_planes[c], weight_scales, N_TILE * c)
+
+        def load_bias(c):
+            nc.sync.dma_start(out=bias_all[c][:], in_=bias[N_TILE * c : N_TILE * (c + 1)].partition_broadcast(P))
+
+        def load_w_block(c):
+            load_w_scales(c)
+            load_w_codes(c, 0)
+            load_bias(c)
+
+        def one_pass(acc, c, t, g, n0, n1):
+            for i, (first, n) in enumerate(X_CHUNKS):
+                if first <= t < first + n:
+                    m0 = M_TILE * (t - first)
+                    lhsT = codes_of_pass(x_codes[i], g)[:, 2 * m0 : 2 * (m0 + M_TILE)]
+                    lhsT_scale = x_planes[i][:, g, m0 : m0 + M_TILE]
+            nc.tensor.matmul_mx(
+                out=acc[:],
+                lhsT=lhsT.bitcast(FP4X4),
+                lhsT_scale=lhsT_scale,
+                rhs=codes_of_pass(w_codes[c], g)[:, 2 * n0 : 2 * n1].bitcast(FP4X4),
+                rhs_scale=w_planes[c][:, g, n0:n1],
+                start=(g == 0),
+                stop=(g == PASSES - 1),
+            )
+
+        def finish(acc, c, t, n0, n1):
+            res = stage.tile([M_TILE, n1 - n0], F32, tag="res")
+            nc.vector.tensor_tensor(out=res[:], in0=acc[:], in1=bias_all[c][:, n0:n1], op=mybir.AluOpType.add)
+            nc.scalar.dma_start(
+                out=out_rows[M_TILE * t : M_TILE * (t + 1), N_TILE * c + n0 : N_TILE * c + n1], in_=res[:]
+            )
+
+        nc.gpsimd.memset(zeros[:], 0.0)
+        zero_plane(w_planes[0])
+        for plane in x_planes:
+            zero_plane(plane)
+        for c in range(1, AHEAD):
+            zero_plane(w_planes[c])
+
+        load_x_codes(0, 0)
+        load_w_codes(0, 0)
+        load_w_scales(0)
+        load_x_scales(0)
+        for j in range(1, len(HEAD_PASSES)):
+            load_w_codes(0, j)
+            load_x_codes(0, j)
+        load_bias(0)
+        for i in range(1, len(X_CHUNKS)):
+            load_x_scales(i)
+            load_x_codes(i, 0)
+        for c in range(1, AHEAD):
+            load_w_block(c)
+
+        warm = psum.tile([M_TILE, N_TILE], F32, tag="acc")
+        for i in range(WARM_MATMULS):
+            nc.tensor.matmul(out=warm[:], lhsT=zeros[:, 0:M_TILE], rhs=zeros[:], start=True, stop=True)
+
+        for c in range(C_BLOCKS):
+            if c + AHEAD < C_BLOCKS:
+                zero_plane(w_planes[c + AHEAD])
+                load_w_block(c + AHEAD)
+            if c == 0:
+                accs = [psum.tile([M_TILE, N_TILE], F32, tag="acc", name="acc_head%d" % t) for t in range(HEAD_TILES)]
+                for g in range(PASSES):
+                    for t in range(HEAD_TILES):
+                        one_pass(accs[t], c, t, g, 0, N_TILE)
+                for t in range(HEAD_TILES):
+                    finish(accs[t], c, t, 0, N_TILE)
+            for t in range(HEAD_TILES if c == 0 else 0, T_TILES):
+                widths = LAST_WIDTHS if (c == C_BLOCKS - 1 and t == T_TILES - 1) else (N_TILE,)
+                n0 = 0
+                for width in widths:
+                    acc = psum.tile([M_TILE, width], F32, tag="acc")
+                    for g in range(PASSES):
+                        one_pass(acc, c, t, g, n0, n0 + width)
+                    finish(acc, c, t, n0, n0 + width)
+                    n0 += width

@@ -18,12 +18,12 @@ N_TILE = 512
 T_TILES = TOKENS // M_TILE
 C_BLOCKS = CHANNELS // N_TILE
 
-X_CHUNKS = ((0, 4), (4, 4), (8, 8))
+X_CHUNKS = ((0, 8), (8, 8))
 HEAD_TILES = X_CHUNKS[0][1]
 ALL_PASSES = ((0, PASSES),)
 HEAD_PASSES = ((0, 1), (1, 2), (2, PASSES))
 AHEAD = 2
-WARM_MATMULS = 6
+WARM_MATMULS = 8
 LAST_WIDTHS = (256, 256)
 
 
@@ -124,7 +124,7 @@ def tile_tiledlinear_kernel(tc, input_words, input_scales, weight_words, weight_
                 out=out_rows[M_TILE * t : M_TILE * (t + 1), N_TILE * c + n0 : N_TILE * c + n1], in_=res[:]
             )
 
-        nc.gpsimd.memset(zeros[:], 0.0)
+        nc.vector.memset(zeros[:], 0.0)
         zero_plane(w_planes[0])
         for plane in x_planes:
             zero_plane(plane)
@@ -138,10 +138,10 @@ def tile_tiledlinear_kernel(tc, input_words, input_scales, weight_words, weight_
         for j in range(1, len(HEAD_PASSES)):
             load_w_codes(0, j)
             load_x_codes(0, j)
-        load_bias(0)
         for i in range(1, len(X_CHUNKS)):
             load_x_scales(i)
             load_x_codes(i, 0)
+        load_bias(0)
         for c in range(1, AHEAD):
             load_w_block(c)
 

@@ -24,6 +24,7 @@ ALL_PASSES = ((0, PASSES),)
 HEAD_PASSES = ((0, 1), (1, 2), (2, PASSES))
 AHEAD = 2
 WARM_MATMULS = 8
+X_CODES_PAD, X_SCALES_PAD, W_CODES_PAD, W_SCALES_PAD = 0, 64, 128, 192
 LAST_WIDTHS = (256, 256)
 
 
@@ -37,11 +38,12 @@ def tile_tiledlinear_kernel(tc, input_words, input_scales, weight_words, weight_
         psum = ctx.enter_context(tc.psum_pool(name="psum", bufs=8))
         ctx.enter_context(tc.manual_schedule())
 
-        def code_tiles(name, width, pass_ranges):
-            return [
-                (g0, g1, keep.tile([P, g1 - g0, width], U8, name="%s_%d" % (name, g0), align_bytes=64))
-                for g0, g1 in pass_ranges
-            ]
+        def mx_tile(name, passes, width, pad):
+            flat = keep.tile([P, pad + passes * width], U8, name=name, align_bytes=256)
+            return flat[:, pad : pad + passes * width].rearrange("p (g n) -> p g n", g=passes)
+
+        def code_tiles(name, width, pass_ranges, pad):
+            return [(g0, g1, mx_tile("%s_%d" % (name, g0), g1 - g0, width, pad)) for g0, g1 in pass_ranges]
 
         def load_codes(tiles, i, words, b0):
             g0, g1, codes = tiles[i]
@@ -56,8 +58,8 @@ def tile_tiledlinear_kernel(tc, input_words, input_scales, weight_words, weight_
                     found = codes[:, g - g0, :]
             return found
 
-        def plane_tile(name, width):
-            return keep.tile([P, PASSES, width], U8, name=name, align_bytes=64)
+        def plane_tile(name, width, pad):
+            return mx_tile(name, PASSES, width, pad)
 
         def zero_plane(plane):
             nc.vector.memset(plane[:].bitcast(I32), 0)
@@ -70,14 +72,14 @@ def tile_tiledlinear_kernel(tc, input_words, input_scales, weight_words, weight_
                 )
 
         x_codes = [
-            code_tiles("x_codes%d" % i, 2 * M_TILE * n, HEAD_PASSES if i == 0 else ALL_PASSES)
+            code_tiles("x_codes%d" % i, 2 * M_TILE * n, HEAD_PASSES if i == 0 else ALL_PASSES, X_CODES_PAD)
             for i, (first, n) in enumerate(X_CHUNKS)
         ]
-        x_planes = [plane_tile("x_plane%d" % i, M_TILE * n) for i, (first, n) in enumerate(X_CHUNKS)]
+        x_planes = [plane_tile("x_plane%d" % i, M_TILE * n, X_SCALES_PAD) for i, (first, n) in enumerate(X_CHUNKS)]
         w_codes = [
-            code_tiles("w_codes%d" % c, 2 * N_TILE, HEAD_PASSES if c == 0 else ALL_PASSES) for c in range(C_BLOCKS)
+            code_tiles("w_codes%d" % c, 2 * N_TILE, HEAD_PASSES if c == 0 else ALL_PASSES, W_CODES_PAD) for c in range(C_BLOCKS)
         ]
-        w_planes = [plane_tile("w_plane%d" % c, N_TILE) for c in range(C_BLOCKS)]
+        w_planes = [plane_tile("w_plane%d" % c, N_TILE, W_SCALES_PAD) for c in range(C_BLOCKS)]
         bias_all = [keep.tile([P, N_TILE], BF16, name="bias%d" % c) for c in range(C_BLOCKS)]
         zeros = keep.tile([P, N_TILE], BF16, name="zeros")
 

@@ -22,6 +22,7 @@ X_CHUNKS = ((0, 8), (8, 8))
 HEAD_TILES = X_CHUNKS[0][1]
 ALL_PASSES = ((0, PASSES),)
 HEAD_PASSES = ((0, 1), (1, 2), (2, PASSES))
+FIRST_TILES = 4
 AHEAD = 2
 WARM_MATMULS = 8
 X_CODES_PAD, X_SCALES_PAD, W_CODES_PAD, W_SCALES_PAD = 0, 64, 128, 192
@@ -58,6 +59,12 @@ def tile_tiledlinear_kernel(tc, input_words, input_scales, weight_words, weight_
                     found = codes[:, g - g0, :]
             return found
 
+        def load_scale_rows(plane, scales, n0, r):
+            nc.sync.dma_start(
+                out=plane[r:P:32, :, :].bitcast(I32),
+                in_=scales[:, r:16:4, n0 : n0 + plane.shape[2]].rearrange("g q n -> q g n").bitcast(I32),
+            )
+
         def plane_tile(name, width, pad):
             return mx_tile(name, PASSES, width, pad)
 
@@ -66,15 +73,13 @@ def tile_tiledlinear_kernel(tc, input_words, input_scales, weight_words, weight_
 
         def load_scales(plane, scales, n0):
             for r in range(4):
-                nc.sync.dma_start(
-                    out=plane[r:P:32, :, :].bitcast(I32),
-                    in_=scales[:, r:16:4, n0 : n0 + plane.shape[2]].rearrange("g q n -> q g n").bitcast(I32),
-                )
+                load_scale_rows(plane, scales, n0, r)
 
         x_codes = [
-            code_tiles("x_codes%d" % i, 2 * M_TILE * n, HEAD_PASSES if i == 0 else ALL_PASSES, X_CODES_PAD)
+            code_tiles("x_codes%d" % i, 2 * M_TILE * n, HEAD_PASSES[1:] if i == 0 else ALL_PASSES, X_CODES_PAD)
             for i, (first, n) in enumerate(X_CHUNKS)
         ]
+        x_first = [mx_tile("x_first%d" % h, 1, 2 * M_TILE * FIRST_TILES, X_CODES_PAD) for h in range(HEAD_TILES // FIRST_TILES)]
         x_planes = [plane_tile("x_plane%d" % i, M_TILE * n, X_SCALES_PAD) for i, (first, n) in enumerate(X_CHUNKS)]
         w_codes = [
             code_tiles("w_codes%d" % c, 2 * N_TILE, HEAD_PASSES if c == 0 else ALL_PASSES, W_CODES_PAD) for c in range(C_BLOCKS)
@@ -85,6 +90,13 @@ def tile_tiledlinear_kernel(tc, input_words, input_scales, weight_words, weight_
 
         def load_x_codes(i, j):
             load_codes(x_codes[i], j, input_words, 2 * M_TILE * X_CHUNKS[i][0])
+
+        def load_x_first(h):
+            width = 2 * M_TILE * FIRST_TILES
+            nc.sync.dma_start(
+                out=x_first[h][:].bitcast(I32),
+                in_=input_words[0:1, :, width * h : width * (h + 1)].rearrange("g p n -> p g n").bitcast(I32),
+            )
 
         def load_x_scales(i):
             load_scales(x_planes[i], input_scales, M_TILE * X_CHUNKS[i][0])
@@ -107,8 +119,12 @@ def tile_tiledlinear_kernel(tc, input_words, input_scales, weight_words, weight_
             for i, (first, n) in enumerate(X_CHUNKS):
                 if first <= t < first + n:
                     m0 = M_TILE * (t - first)
-                    lhsT = codes_of_pass(x_codes[i], g)[:, 2 * m0 : 2 * (m0 + M_TILE)]
                     lhsT_scale = x_planes[i][:, g, m0 : m0 + M_TILE]
+                    if g == 0 and t < HEAD_TILES:
+                        m1 = M_TILE * (t % FIRST_TILES)
+                        lhsT = x_first[t // FIRST_TILES][:, 0, 2 * m1 : 2 * (m1 + M_TILE)]
+                    else:
+                        lhsT = codes_of_pass(x_codes[i], g)[:, 2 * m0 : 2 * (m0 + M_TILE)]
             nc.tensor.matmul_mx(
                 out=acc[:],
                 lhsT=lhsT.bitcast(FP4X4),
@@ -133,13 +149,18 @@ def tile_tiledlinear_kernel(tc, input_words, input_scales, weight_words, weight_
         for c in range(1, AHEAD):
             zero_plane(w_planes[c])
 
-        load_x_codes(0, 0)
+        load_x_first(0)
         load_w_codes(0, 0)
-        load_w_scales(0)
+        for r in (0, 1):
+            load_scale_rows(w_planes[0], weight_scales, 0, r)
         load_x_scales(0)
+        for r in (2, 3):
+            load_scale_rows(w_planes[0], weight_scales, 0, r)
+        for h in range(1, len(x_first)):
+            load_x_first(h)
         for j in range(1, len(HEAD_PASSES)):
             load_w_codes(0, j)
-            load_x_codes(0, j)
+            load_x_codes(0, j - 1)
         for i in range(1, len(X_CHUNKS)):
             load_x_scales(i)
             load_x_codes(i, 0)

@@ -35,7 +35,7 @@ def tile_tiledlinear_kernel(tc, input_words, input_scales, weight_words, weight_
 
     with ExitStack() as ctx:
         keep = ctx.enter_context(tc.tile_pool(name="keep", bufs=1))
-        stage = ctx.enter_context(tc.tile_pool(name="stage", bufs=6))
+        stage = ctx.enter_context(tc.tile_pool(name="stage", bufs=16))
         psum = ctx.enter_context(tc.psum_pool(name="psum", bufs=8))
         ctx.enter_context(tc.manual_schedule())
 
@@ -87,6 +87,7 @@ def tile_tiledlinear_kernel(tc, input_words, input_scales, weight_words, weight_
         w_planes = [plane_tile("w_plane%d" % c, N_TILE, W_SCALES_PAD) for c in range(C_BLOCKS)]
         bias_all = [keep.tile([P, N_TILE], BF16, name="bias%d" % c) for c in range(C_BLOCKS)]
         zeros = keep.tile([P, N_TILE], BF16, name="zeros")
+        table_dummy = keep.tile([P, 1], BF16, name="table_dummy")
 
         def load_x_codes(i, j):
             load_codes(x_codes[i], j, input_words, 2 * M_TILE * X_CHUNKS[i][0])
@@ -135,14 +136,18 @@ def tile_tiledlinear_kernel(tc, input_words, input_scales, weight_words, weight_
                 stop=(g == PASSES - 1),
             )
 
-        def finish(acc, c, t, n0, n1):
-            res = stage.tile([M_TILE, n1 - n0], F32, tag="res")
-            nc.vector.tensor_tensor(out=res[:], in0=acc[:], in1=bias_all[c][:, n0:n1], op=mybir.AluOpType.add)
+        def store(res, c, t, n0, n1):
             nc.scalar.dma_start(
                 out=out_rows[M_TILE * t : M_TILE * (t + 1), N_TILE * c + n0 : N_TILE * c + n1], in_=res[:]
             )
 
+        def finish(acc, c, t, n0, n1):
+            res = stage.tile([M_TILE, n1 - n0], F32, tag="res")
+            nc.vector.tensor_tensor(out=res[:], in0=acc[:], in1=bias_all[c][:, n0:n1], op=mybir.AluOpType.add)
+            store(res, c, t, n0, n1)
+
         nc.vector.memset(zeros[:], 0.0)
+        nc.scalar.copy(out=table_dummy[:], in_=zeros[:, 0:1])
         zero_plane(w_planes[0])
         for plane in x_planes:
             zero_plane(plane)
@@ -181,8 +186,12 @@ def tile_tiledlinear_kernel(tc, input_words, input_scales, weight_words, weight_
                 for g in range(PASSES):
                     for t in range(HEAD_TILES):
                         one_pass(accs[t], c, t, g, 0, N_TILE)
+                bare = [stage.tile([M_TILE, N_TILE], F32, tag="res", name="bare%d" % t) for t in range(HEAD_TILES)]
                 for t in range(HEAD_TILES):
-                    finish(accs[t], c, t, 0, N_TILE)
+                    nc.scalar.copy(out=bare[t][:], in_=accs[t][:])
+                for t in range(HEAD_TILES):
+                    nc.vector.tensor_tensor(out=bare[t][:], in0=bare[t][:], in1=bias_all[c][:], op=mybir.AluOpType.add)
+                    store(bare[t], c, t, 0, N_TILE)
             for t in range(HEAD_TILES if c == 0 else 0, T_TILES):
                 widths = LAST_WIDTHS if (c == C_BLOCKS - 1 and t == T_TILES - 1) else (N_TILE,)
                 n0 = 0

@@ -23,7 +23,8 @@ HEAD_TILES = X_CHUNKS[0][1]
 ALL_PASSES = ((0, PASSES),)
 HEAD_PASSES = ((0, 1), (1, 2), (2, PASSES))
 FIRST_TILES = 4
-AHEAD = 2
+OWN_PLANES = 2
+W_BUFFERS = 2
 WARM_MATMULS = 8
 X_CODES_PAD, X_SCALES_PAD, W_CODES_PAD, W_SCALES_PAD = 0, 64, 128, 192
 LAST_WIDTHS = (256, 256)
@@ -36,6 +37,7 @@ def tile_tiledlinear_kernel(tc, input_words, input_scales, weight_words, weight_
     with ExitStack() as ctx:
         keep = ctx.enter_context(tc.tile_pool(name="keep", bufs=1))
         stage = ctx.enter_context(tc.tile_pool(name="stage", bufs=16))
+        turn = ctx.enter_context(tc.tile_pool(name="turn", bufs=W_BUFFERS))
         psum = ctx.enter_context(tc.psum_pool(name="psum", bufs=8))
         ctx.enter_context(tc.manual_schedule())
 
@@ -81,11 +83,11 @@ def tile_tiledlinear_kernel(tc, input_words, input_scales, weight_words, weight_
         ]
         x_first = [mx_tile("x_first%d" % h, 1, 2 * M_TILE * FIRST_TILES, X_CODES_PAD) for h in range(HEAD_TILES // FIRST_TILES)]
         x_planes = [plane_tile("x_plane%d" % i, M_TILE * n, X_SCALES_PAD) for i, (first, n) in enumerate(X_CHUNKS)]
-        w_codes = [
-            code_tiles("w_codes%d" % c, 2 * N_TILE, HEAD_PASSES if c == 0 else ALL_PASSES, W_CODES_PAD) for c in range(C_BLOCKS)
-        ]
-        w_planes = [plane_tile("w_plane%d" % c, N_TILE, W_SCALES_PAD) for c in range(C_BLOCKS)]
-        bias_all = [keep.tile([P, N_TILE], BF16, name="bias%d" % c) for c in range(C_BLOCKS)]
+        w_codes = [code_tiles("w_codes0", 2 * N_TILE, HEAD_PASSES, W_CODES_PAD)]
+        w_plane_rest = plane_tile("w_plane_rest", N_TILE * (C_BLOCKS - OWN_PLANES), W_SCALES_PAD)
+        w_planes = [plane_tile("w_plane%d" % c, N_TILE, W_SCALES_PAD) for c in range(OWN_PLANES)]
+        w_planes.extend([w_plane_rest[:, :, N_TILE * (c - OWN_PLANES) : N_TILE * (c - OWN_PLANES + 1)] for c in range(OWN_PLANES, C_BLOCKS)])
+        bias_all = [keep.tile([P, N_TILE], BF16, name="bias0")]
         zeros = keep.tile([P, N_TILE], BF16, name="zeros")
         table_dummy = keep.tile([P, 1], BF16, name="table_dummy")
 
@@ -105,14 +107,15 @@ def tile_tiledlinear_kernel(tc, input_words, input_scales, weight_words, weight_
         def load_w_codes(c, j):
             load_codes(w_codes[c], j, weight_words, 2 * N_TILE * c)
 
-        def load_w_scales(c):
-            load_scales(w_planes[c], weight_scales, N_TILE * c)
-
         def load_bias(c):
             nc.sync.dma_start(out=bias_all[c][:], in_=bias[N_TILE * c : N_TILE * (c + 1)].partition_broadcast(P))
 
         def load_w_block(c):
-            load_w_scales(c)
+            nbytes = W_CODES_PAD + PASSES * 2 * N_TILE
+            flat = turn.tile([P, nbytes], U8, tag="w_codes", align_bytes=256)
+            w_codes.append([(0, PASSES, flat[:, W_CODES_PAD:nbytes].rearrange("p (g n) -> p g n", g=PASSES))])
+            bias_c = turn.tile([P, N_TILE], BF16, tag="bias")
+            bias_all.append(bias_c)
             load_w_codes(c, 0)
             load_bias(c)
 
@@ -151,8 +154,9 @@ def tile_tiledlinear_kernel(tc, input_words, input_scales, weight_words, weight_
         zero_plane(w_planes[0])
         for plane in x_planes:
             zero_plane(plane)
-        for c in range(1, AHEAD):
+        for c in range(1, OWN_PLANES):
             zero_plane(w_planes[c])
+        zero_plane(w_plane_rest)
 
         load_x_first(0)
         load_w_codes(0, 0)
@@ -170,7 +174,11 @@ def tile_tiledlinear_kernel(tc, input_words, input_scales, weight_words, weight_
             load_x_scales(i)
             load_x_codes(i, 0)
         load_bias(0)
-        for c in range(1, AHEAD):
+        for c in range(1, OWN_PLANES):
+            load_scales(w_planes[c], weight_scales, N_TILE * c)
+            load_w_block(c)
+        load_scales(w_plane_rest, weight_scales, N_TILE * OWN_PLANES)
+        for c in range(OWN_PLANES, 1 + W_BUFFERS):
             load_w_block(c)
 
         warm = psum.tile([M_TILE, N_TILE], F32, tag="acc")
@@ -178,9 +186,8 @@ def tile_tiledlinear_kernel(tc, input_words, input_scales, weight_words, weight_
             nc.tensor.matmul(out=warm[:], lhsT=zeros[:, 0:M_TILE], rhs=zeros[:], start=True, stop=True)
 
         for c in range(C_BLOCKS):
-            if c + AHEAD < C_BLOCKS:
-                zero_plane(w_planes[c + AHEAD])
-                load_w_block(c + AHEAD)
+            if W_BUFFERS <= c < C_BLOCKS - 1:
+                load_w_block(c + 1)
             if c == 0:
                 accs = [psum.tile([M_TILE, N_TILE], F32, tag="acc", name="acc_head%d" % t) for t in range(HEAD_TILES)]
                 for g in range(PASSES):

@@ -27,6 +27,9 @@ OWN_PLANES = 2
 W_BUFFERS = 2
 WARM_MATMULS = 8
 X_CODES_PAD, X_SCALES_PAD, W_CODES_PAD, W_SCALES_PAD = 0, 64, 128, 192
+STORE_TILES = 4
+GROUP_BUFFERS = 6
+FINE_BUFFERS = 5
 LAST_WIDTHS = (256, 256)
 
 
@@ -36,7 +39,8 @@ def tile_tiledlinear_kernel(tc, input_words, input_scales, weight_words, weight_
 
     with ExitStack() as ctx:
         keep = ctx.enter_context(tc.tile_pool(name="keep", bufs=1))
-        stage = ctx.enter_context(tc.tile_pool(name="stage", bufs=16))
+        stage = ctx.enter_context(tc.tile_pool(name="stage", bufs=GROUP_BUFFERS))
+        fine = ctx.enter_context(tc.tile_pool(name="fine", bufs=FINE_BUFFERS))
         turn = ctx.enter_context(tc.tile_pool(name="turn", bufs=W_BUFFERS))
         psum = ctx.enter_context(tc.psum_pool(name="psum", bufs=8))
         ctx.enter_context(tc.manual_schedule())
@@ -144,10 +148,29 @@ def tile_tiledlinear_kernel(tc, input_words, input_scales, weight_words, weight_
                 out=out_rows[M_TILE * t : M_TILE * (t + 1), N_TILE * c + n0 : N_TILE * c + n1], in_=res[:]
             )
 
+        groups = []
+
+        def group_slot(t):
+            if t % STORE_TILES == 0:
+                groups.append(stage.tile([M_TILE, STORE_TILES, N_TILE], F32, tag="res", name="res_group"))
+            return groups[-1][:, t % STORE_TILES, :]
+
+        def store_group(c, t):
+            if t % STORE_TILES == STORE_TILES - 1:
+                t0 = t + 1 - STORE_TILES
+                nc.scalar.dma_start(
+                    out=out_rows[M_TILE * t0 : M_TILE * (t + 1), N_TILE * c : N_TILE * (c + 1)].rearrange("(j p) n -> p j n", p=M_TILE),
+                    in_=groups[-1][:],
+                )
+
         def finish(acc, c, t, n0, n1):
-            res = stage.tile([M_TILE, n1 - n0], F32, tag="res")
-            nc.vector.tensor_tensor(out=res[:], in0=acc[:], in1=bias_all[c][:, n0:n1], op=mybir.AluOpType.add)
-            store(res, c, t, n0, n1)
+            if c == C_BLOCKS - 1 and t >= T_TILES - STORE_TILES:
+                res = fine.tile([M_TILE, n1 - n0], F32, tag="res_fine")
+                nc.vector.tensor_tensor(out=res[:], in0=acc[:], in1=bias_all[c][:, n0:n1], op=mybir.AluOpType.add)
+                store(res, c, t, n0, n1)
+            else:
+                nc.vector.tensor_tensor(out=group_slot(t), in0=acc[:], in1=bias_all[c][:, n0:n1], op=mybir.AluOpType.add)
+                store_group(c, t)
 
         nc.vector.memset(zeros[:], 0.0)
         nc.scalar.copy(out=table_dummy[:], in_=zeros[:, 0:1])
@@ -193,12 +216,14 @@ def tile_tiledlinear_kernel(tc, input_words, input_scales, weight_words, weight_
                 for g in range(PASSES):
                     for t in range(HEAD_TILES):
                         one_pass(accs[t], c, t, g, 0, N_TILE)
-                bare = [stage.tile([M_TILE, N_TILE], F32, tag="res", name="bare%d" % t) for t in range(HEAD_TILES)]
+                bare = [group_slot(t) for t in range(HEAD_TILES)]
+                head_groups = list(groups)
                 for t in range(HEAD_TILES):
-                    nc.scalar.copy(out=bare[t][:], in_=accs[t][:])
+                    nc.scalar.copy(out=bare[t], in_=accs[t][:])
                 for t in range(HEAD_TILES):
-                    nc.vector.tensor_tensor(out=bare[t][:], in0=bare[t][:], in1=bias_all[c][:], op=mybir.AluOpType.add)
-                    store(bare[t], c, t, 0, N_TILE)
+                    nc.vector.tensor_tensor(out=bare[t], in0=bare[t], in1=bias_all[c][:], op=mybir.AluOpType.add)
+                    groups.append(head_groups[t // STORE_TILES])
+                    store_group(c, t)
             for t in range(HEAD_TILES if c == 0 else 0, T_TILES):
                 widths = LAST_WIDTHS if (c == C_BLOCKS - 1 and t == T_TILES - 1) else (N_TILE,)
                 n0 = 0

from contextlib import ExitStack

import concourse.mybir as mybir

TOKENS, FEATURES, CHANNELS = 2048, 2048, 4096
FLOPS = 2 * TOKENS * FEATURES * CHANNELS

F32 = mybir.dt.float32
BF16 = mybir.dt.bfloat16
I32 = mybir.dt.int32
U8 = mybir.dt.uint8
FP4X4 = mybir.dt.float4_e2m1fn_x4

P = 128
PASSES = FEATURES // 512
M_TILE = 128
N_TILE = 512
T_TILES = TOKENS // M_TILE
C_BLOCKS = CHANNELS // N_TILE

X_CHUNKS = ((0, 8), (8, 8))
HEAD_TILES = X_CHUNKS[0][1]
ALL_PASSES = ((0, PASSES),)
HEAD_PASSES = ((0, 1), (1, 2), (2, PASSES))
FIRST_TILES = 4
OWN_PLANES = 2
W_BUFFERS = 2
WARM_MATMULS = 8
X_CODES_PAD, X_SCALES_PAD, W_CODES_PAD, W_SCALES_PAD = 0, 64, 128, 192
STORE_TILES = 4
GROUP_BUFFERS = 6
FINE_BUFFERS = 5
LAST_WIDTHS = (256, 256)


def tile_tiledlinear_kernel(tc, input_words, input_scales, weight_words, weight_scales, bias, out):
    nc = tc.nc
    out_rows = out.flatten_outer_dims()

    with ExitStack() as ctx:
        keep = ctx.enter_context(tc.tile_pool(name="keep", bufs=1))
        stage = ctx.enter_context(tc.tile_pool(name="stage", bufs=GROUP_BUFFERS))
        fine = ctx.enter_context(tc.tile_pool(name="fine", bufs=FINE_BUFFERS))
        turn = ctx.enter_context(tc.tile_pool(name="turn", bufs=W_BUFFERS))
        psum = ctx.enter_context(tc.psum_pool(name="psum", bufs=8))
        ctx.enter_context(tc.manual_schedule())

        def mx_tile(name, passes, width, pad):
            flat = keep.tile([P, pad + passes * width], U8, name=name, align_bytes=256)
            return flat[:, pad : pad + passes * width].rearrange("p (g n) -> p g n", g=passes)

        def code_tiles(name, width, pass_ranges, pad):
            return [(g0, g1, mx_tile("%s_%d" % (name, g0), g1 - g0, width, pad)) for g0, g1 in pass_ranges]

        def load_codes(tiles, i, words, b0):
            g0, g1, codes = tiles[i]
            nc.sync.dma_start(
                out=codes[:].bitcast(I32),
                in_=words[g0:g1, :, b0 : b0 + codes.shape[2]].rearrange("g p n -> p g n").bitcast(I32),
            )

        def codes_of_pass(tiles, g):
            for g0, g1, codes in tiles:
                if g0 <= g < g1:
                    found = codes[:, g - g0, :]
            return found

        def load_scale_rows(plane, scales, n0, r):
            nc.sync.dma_start(
                out=plane[r:P:32, :, :].bitcast(I32),
                in_=scales[:, r:16:4, n0 : n0 + plane.shape[2]].rearrange("g q n -> q g n").bitcast(I32),
            )

        def plane_tile(name, width, pad):
            return mx_tile(name, PASSES, width, pad)

        def zero_plane(plane):
            nc.vector.memset(plane[:].bitcast(I32), 0)

        def load_scales(plane, scales, n0):
            for r in range(4):
                load_scale_rows(plane, scales, n0, r)

        x_codes = [
            code_tiles("x_codes%d" % i, 2 * M_TILE * n, HEAD_PASSES[1:] if i == 0 else ALL_PASSES, X_CODES_PAD)
            for i, (first, n) in enumerate(X_CHUNKS)
        ]
        x_first = [mx_tile("x_first%d" % h, 1, 2 * M_TILE * FIRST_TILES, X_CODES_PAD) for h in range(HEAD_TILES // FIRST_TILES)]
        x_planes = [plane_tile("x_plane%d" % i, M_TILE * n, X_SCALES_PAD) for i, (first, n) in enumerate(X_CHUNKS)]
        w_codes = [code_tiles("w_codes0", 2 * N_TILE, HEAD_PASSES, W_CODES_PAD)]
        w_plane_rest = plane_tile("w_plane_rest", N_TILE * (C_BLOCKS - OWN_PLANES), W_SCALES_PAD)
        w_planes = [plane_tile("w_plane%d" % c, N_TILE, W_SCALES_PAD) for c in range(OWN_PLANES)]
        w_planes.extend([w_plane_rest[:, :, N_TILE * (c - OWN_PLANES) : N_TILE * (c - OWN_PLANES + 1)] for c in range(OWN_PLANES, C_BLOCKS)])
        bias_all = [keep.tile([P, N_TILE], BF16, name="bias0")]
        zeros = keep.tile([P, N_TILE], BF16, name="zeros")
        table_dummy = keep.tile([P, 1], BF16, name="table_dummy")

        def load_x_codes(i, j):
            load_codes(x_codes[i], j, input_words, 2 * M_TILE * X_CHUNKS[i][0])

        def load_x_first(h):
            width = 2 * M_TILE * FIRST_TILES
            nc.sync.dma_start(
                out=x_first[h][:].bitcast(I32),
                in_=input_words[0:1, :, width * h : width * (h + 1)].rearrange("g p n -> p g n").bitcast(I32),
            )

        def load_x_scales(i):
            load_scales(x_planes[i], input_scales, M_TILE * X_CHUNKS[i][0])

        def load_w_codes(c, j):
            load_codes(w_codes[c], j, weight_words, 2 * N_TILE * c)

        def load_bias(c):
            nc.sync.dma_start(out=bias_all[c][:], in_=bias[N_TILE * c : N_TILE * (c + 1)].partition_broadcast(P))

        def load_w_block(c):
            nbytes = W_CODES_PAD + PASSES * 2 * N_TILE
            flat = turn.tile([P, nbytes], U8, tag="w_codes", align_bytes=256)
            w_codes.append([(0, PASSES, flat[:, W_CODES_PAD:nbytes].rearrange("p (g n) -> p g n", g=PASSES))])
            bias_c = turn.tile([P, N_TILE], BF16, tag="bias")
            bias_all.append(bias_c)
            load_w_codes(c, 0)
            load_bias(c)

        def one_pass(acc, c, t, g, n0, n1):
            for i, (first, n) in enumerate(X_CHUNKS):
                if first <= t < first + n:
                    m0 = M_TILE * (t - first)
                    lhsT_scale = x_planes[i][:, g, m0 : m0 + M_TILE]
                    if g == 0 and t < HEAD_TILES:
                        m1 = M_TILE * (t % FIRST_TILES)
                        lhsT = x_first[t // FIRST_TILES][:, 0, 2 * m1 : 2 * (m1 + M_TILE)]
                    else:
                        lhsT = codes_of_pass(x_codes[i], g)[:, 2 * m0 : 2 * (m0 + M_TILE)]
            nc.tensor.matmul_mx(
                out=acc[:],
                lhsT=lhsT.bitcast(FP4X4),
                lhsT_scale=lhsT_scale,
                rhs=codes_of_pass(w_codes[c], g)[:, 2 * n0 : 2 * n1].bitcast(FP4X4),
                rhs_scale=w_planes[c][:, g, n0:n1],
                start=(g == 0),
                stop=(g == PASSES - 1),
            )

        def store(res, c, t, n0, n1):
            nc.scalar.dma_start(
                out=out_rows[M_TILE * t : M_TILE * (t + 1), N_TILE * c + n0 : N_TILE * c + n1], in_=res[:]
            )

        groups = []

        def group_slot(t):
            if t % STORE_TILES == 0:
                groups.append(stage.tile([M_TILE, STORE_TILES, N_TILE], F32, tag="res", name="res_group"))
            return groups[-1][:, t % STORE_TILES, :]

        def store_group(c, t):
            if t % STORE_TILES == STORE_TILES - 1:
                t0 = t + 1 - STORE_TILES
                nc.scalar.dma_start(
                    out=out_rows[M_TILE * t0 : M_TILE * (t + 1), N_TILE * c : N_TILE * (c + 1)].rearrange("(j p) n -> p j n", p=M_TILE),
                    in_=groups[-1][:],
                )

        def finish(acc, c, t, n0, n1):
            if c == C_BLOCKS - 1 and t >= T_TILES - STORE_TILES:
                res = fine.tile([M_TILE, n1 - n0], F32, tag="res_fine")
                nc.vector.tensor_tensor(out=res[:], in0=acc[:], in1=bias_all[c][:, n0:n1], op=mybir.AluOpType.add)
                store(res, c, t, n0, n1)
            else:
                nc.vector.tensor_tensor(out=group_slot(t), in0=acc[:], in1=bias_all[c][:, n0:n1], op=mybir.AluOpType.add)
                store_group(c, t)

        nc.vector.memset(zeros[:], 0.0)
        nc.scalar.copy(out=table_dummy[:], in_=zeros[:, 0:1])
        zero_plane(w_planes[0])
        for plane in x_planes:
            zero_plane(plane)
        for c in range(1, OWN_PLANES):
            zero_plane(w_planes[c])
        zero_plane(w_plane_rest)

        load_x_first(0)
        load_w_codes(0, 0)
        for r in (0, 1):
            load_scale_rows(w_planes[0], weight_scales, 0, r)
        load_x_scales(0)
        for r in (2, 3):
            load_scale_rows(w_planes[0], weight_scales, 0, r)
        for h in range(1, len(x_first)):
            load_x_first(h)
        for j in range(1, len(HEAD_PASSES)):
            load_w_codes(0, j)
            load_x_codes(0, j - 1)
        for i in range(1, len(X_CHUNKS)):
            load_x_scales(i)
            load_x_codes(i, 0)
        load_bias(0)
        for c in range(1, OWN_PLANES):
            load_scales(w_planes[c], weight_scales, N_TILE * c)
            load_w_block(c)
        load_scales(w_plane_rest, weight_scales, N_TILE * OWN_PLANES)
        for c in range(OWN_PLANES, 1 + W_BUFFERS):
            load_w_block(c)

        warm = psum.tile([M_TILE, N_TILE], F32, tag="acc")
        for i in range(WARM_MATMULS):
            nc.tensor.matmul(out=warm[:], lhsT=zeros[:, 0:M_TILE], rhs=zeros[:], start=True, stop=True)

        for c in range(C_BLOCKS):
            if W_BUFFERS <= c < C_BLOCKS - 1:
                load_w_block(c + 1)
            if c == 0:
                accs = [psum.tile([M_TILE, N_TILE], F32, tag="acc", name="acc_head%d" % t) for t in range(HEAD_TILES)]
                for g in range(PASSES):
                    for t in range(HEAD_TILES):
                        one_pass(accs[t], c, t, g, 0, N_TILE)
                bare = [group_slot(t) for t in range(HEAD_TILES)]
                head_groups = list(groups)
                for t in range(HEAD_TILES):
                    nc.scalar.copy(out=bare[t], in_=accs[t][:])
                for t in range(HEAD_TILES):
                    nc.vector.tensor_tensor(out=bare[t], in0=bare[t], in1=bias_all[c][:], op=mybir.AluOpType.add)
                    groups.append(head_groups[t // STORE_TILES])
                    store_group(c, t)
            for t in range(HEAD_TILES if c == 0 else 0, T_TILES):
                widths = LAST_WIDTHS if (c == C_BLOCKS - 1 and t == T_TILES - 1) else (N_TILE,)
                n0 = 0
                for width in widths:
                    acc = psum.tile([M_TILE, width], F32, tag="acc")
                    for g in range(PASSES):
                        one_pass(acc, c, t, g, n0, n0 + width)
                    finish(acc, c, t, n0, n0 + width)
                    n0 += width
